import numpy as np
import ml_dtypes


def mxq(x, axis, fmt="e4m3"):
    dtype, down = {"e4m3": (ml_dtypes.float8_e4m3fn, 7), "e5m2": (ml_dtypes.float8_e5m2, 14)}[fmt]
    v = np.moveaxis(np.asarray(x, np.float32).astype(ml_dtypes.bfloat16).astype(np.float64), axis, -1)
    blocks = v.reshape(v.shape[:-1] + (-1, 32))
    amax = np.abs(blocks).max(-1, keepdims=True)
    byte = np.maximum(np.where(amax > 0, np.frexp(amax)[1] - 1 + 127, 0) - down, 1)
    scale = np.exp2(byte - 127.0)
    codes = (blocks / scale).astype(np.float32).astype(dtype).astype(np.float64)
    return np.moveaxis((codes * scale).reshape(v.shape), -1, axis)


WIDE = False


def mx_kscale(k):
    if not WIDE:
        return np.ones(k)
    levels = np.array([10, -10, 5, -5, 0])
    if k % 512:
        return np.exp2(np.random.permutation(np.resize(levels, k // 32))).repeat(32)
    a = np.empty((k // 512, 16))
    for p in range(k // 512):
        a[p, :8] = np.random.permutation(np.resize(levels, 8))
        for g in range(8):
            far = levels[np.abs(levels - a[p, g]) >= 10]
            a[p, g + 8] = far[np.random.randint(len(far))]
    return np.exp2(a.ravel()).repeat(32)


BF16 = ml_dtypes.bfloat16


def bf(x):
    return np.asarray(x, np.float32).astype(BF16)


def f64(x):
    return np.asarray(x).astype(np.float64)


T, B, D, M = 4, 128, 512, 128
TEMP = 0.1
QS = 0.3
SC = 2.0
MS = SC * TEMP / (QS * np.sqrt(D))
WS = QS * np.sqrt(SC**2 / D + 0.4 / B)


def sigmoid(v):
    return 1.0 / (1.0 + np.exp(-v))


def setup_inputs():
    s = mx_kscale(D)
    return {"queries": bf(np.random.standard_normal((T, B, D)) * QS / s),
            "memory_items": bf(np.random.standard_normal((M, D)) * MS * s),
            "wq": bf(np.random.standard_normal((M, D)) * WS * s),
            "U_w": bf(np.random.standard_normal((D, D)) / (MS * np.sqrt(D)) / s[None, :]),
            "W_w": bf(np.random.standard_normal((D, D)) / (WS * np.sqrt(D)) / s[None, :])}


def reference(queries, memory_items, wq, U_w, W_w):
    q = f64(queries).reshape(T * B, D)
    mem = f64(memory_items)
    w = f64(wq)
    gate = sigmoid((mxq(mem, 1, "e4m3") @ mxq(f64(U_w), 1, "e4m3").T) + (mxq(w, 1, "e4m3") @ mxq(f64(W_w), 1, "e4m3").T))
    m_new = (1.0 - gate) * mem + gate * w
    logits = (mxq(q, 1, "e4m3") @ mxq(m_new, 1, "e4m3").T) / TEMP
    e = np.exp(logits - logits.max(-1, keepdims=True))
    w_att = e / e.sum(-1, keepdims=True)
    return m_new, w_att.reshape(T, B, M)

@@ -1,0 +1,247 @@
+from contextlib import ExitStack
+
+import concourse.mybir as mybir
+from concourse.masks import make_identity
+
+F32 = mybir.dt.float32
+BF16 = mybir.dt.bfloat16
+U32 = mybir.dt.uint32
+U8 = mybir.dt.uint8
+FP8X4 = mybir.dt.float8_e4m3fn_x4
+ACT = mybir.ActivationFunctionType
+ALU = mybir.AluOpType
+AXIS = mybir.AxisListType
+
+P = 128
+D = 512
+PACK = 4
+INV_TEMP = 10.0
+
+FLOPS = 2 * (2 * P * D * D) + 2 * (4 * P) * D * P
+
+
+def tile_gatedmemorymodule_pb_s_kernel(
+    tc, queries, memory_items, wq, U_w, W_w, out_0, out_1
+):
+    nc = tc.nc
+    with ExitStack() as ctx:
+        ctx.enter_context(tc.manual_schedule())
+        keep = ctx.enter_context(tc.tile_pool(name="keep", bufs=1))
+        stage = ctx.enter_context(tc.tile_pool(name="stage", bufs=4))
+        flip_psum = ctx.enter_context(tc.psum_pool(name="flip_psum", bufs=4))
+        half_psum = ctx.enter_context(tc.psum_pool(name="half_psum", bufs=2))
+        back_psum = ctx.enter_context(tc.psum_pool(name="back_psum", bufs=1))
+
+        identity = keep.tile([P, P], F32)
+        make_identity(nc, identity[:])
+
+        zero = keep.tile([P, 1], F32)
+        nc.vector.memset(zero[:], 0.0)
+        warm = keep.tile([P, 1], F32)
+        nc.scalar.activation(out=warm[:], in_=zero[:], func=ACT.Exp)
+
+        slots_sb = keep.tile([P, 2, D], BF16)
+        nc.sync.dma_start(out=slots_sb[:, 0, :], in_=memory_items)
+        nc.sync.dma_start(out=slots_sb[:, 1, :], in_=wq)
+        u_rows = U_w.rearrange("(p u e) d -> u p (e d)", u=2, e=2)
+        w_rows = W_w.rearrange("(p u e) d -> u p (e d)", u=2, e=2)
+        u_sb = keep.tile([P, PACK, D], BF16)
+        w_sb = keep.tile([P, PACK, D], BF16)
+        for u in range(2):
+            ts = slice(2 * u, 2 * u + 2)
+            nc.sync.dma_start(out=u_sb[:, ts, :].rearrange("p e d -> p (e d)"), in_=u_rows[u])
+            nc.sync.dma_start(out=w_sb[:, ts, :].rearrange("p e d -> p (e d)"), in_=w_rows[u])
+        q_rows = queries.rearrange("t b d -> (t b) d").rearrange("(r h i) d -> h r (i d)", h=2, i=2)
+        q_sb = keep.tile([P, PACK, D], BF16)
+        for h in range(2):
+            js = slice(2 * h, 2 * h + 2)
+            nc.sync.dma_start(out=q_sb[:, js, :].rearrange("r i d -> r (i d)"), in_=q_rows[h])
+
+        def transpose_tile(rows_sb, grouped):
+            words = rows_sb.bitcast(F32)
+            flipped = flip_psum.tile([P, 2, P], F32)
+            for u in range(2):
+                nc.tensor.transpose(flipped[:, u, :], words[:, u : 2 * P : 2], identity[:])
+            nc.scalar.copy(
+                out=grouped.rearrange("p r t -> p (r t)").bitcast(F32).rearrange("p (r u) -> p r u", u=2),
+                in_=flipped[:].rearrange("p u r -> p r u"),
+            )
+
+        def quantise(grouped, codes, scales):
+            nc.vector.quantize_mx(
+                out=codes.bitcast(FP8X4), scales=scales, in_=grouped.rearrange("p r t -> p (r t)")
+            )
+
+        slot_codes = keep.tile([P, 2 * P], U32, align_bytes=64)
+        slot_scales = keep.tile([P, 2 * P], U8, align_bytes=64)
+        u_codes = keep.tile([P, PACK * P], U32, align_bytes=64)
+        u_scales = keep.tile([P, PACK * P], U8, align_bytes=64)
+        w_codes = keep.tile([P, PACK * P], U32, align_bytes=64)
+        w_scales = keep.tile([P, PACK * P], U8, align_bytes=64)
+        q_codes = keep.tile([P, PACK * P], U32, align_bytes=64)
+        q_scales = keep.tile([P, PACK * P], U8, align_bytes=64)
+
+        slots_grouped = keep.tile([P, 2, P, PACK], BF16, align_bytes=64)
+        for i in range(2):
+            chunk = slice(i * P, (i + 1) * P)
+            transpose_tile(slots_sb[:, i, :], slots_grouped[:, i, :, :])
+            quantise(slots_grouped[:, i, :, :], slot_codes[:, chunk], slot_scales[:, chunk])
+        mem_planes = slots_grouped[:, 0, :, :].rearrange("p m t -> p t m")
+        wq_planes = slots_grouped[:, 1, :, :].rearrange("p m t -> p t m")
+        diff_planes = keep.tile([P, PACK, P], F32)
+        nc.vector.tensor_tensor(out=diff_planes[:], in0=wq_planes, in1=mem_planes, op=ALU.subtract)
+
+        for u in range(2):
+            for rows, codes, scales in ((u_sb, u_codes, u_scales), (w_sb, w_codes, w_scales)):
+                for t in (2 * u, 2 * u + 1):
+                    chunk = slice(t * P, (t + 1) * P)
+                    grouped = stage.tile([P, P, PACK], BF16, align_bytes=64)
+                    transpose_tile(rows[:, t, :], grouped[:])
+                    quantise(grouped[:], codes[:, chunk], scales[:, chunk])
+
+        gate_halves = []
+        for u in range(2):
+            gate_ps = half_psum.tile([P, 2, P], F32, tag="half")
+            gate_halves.append(gate_ps)
+            for e in range(2):
+                chunk = slice((2 * u + e) * P, (2 * u + e + 1) * P)
+                nc.tensor.matmul_mx(
+                    out=gate_ps[:, e, :],
+                    lhsT=u_codes[:, chunk].bitcast(FP8X4),
+                    lhsT_scale=u_scales[:, chunk],
+                    rhs=slot_codes[:, 0:P].bitcast(FP8X4),
+                    rhs_scale=slot_scales[:, 0:P],
+                    start=True,
+                    stop=False,
+                )
+                nc.tensor.matmul_mx(
+                    out=gate_ps[:, e, :],
+                    lhsT=w_codes[:, chunk].bitcast(FP8X4),
+                    lhsT_scale=w_scales[:, chunk],
+                    rhs=slot_codes[:, P : 2 * P].bitcast(FP8X4),
+                    rhs_scale=slot_scales[:, P : 2 * P],
+                    start=False,
+                    stop=True,
+                )
+
+        tanh_planes = keep.tile([P, PACK, P], F32)
+        for u in range(2):
+            nc.scalar.activation(
+                out=tanh_planes[:, 2 * u : 2 * u + 2, :], in_=gate_halves[u][:], func=ACT.Tanh, scale=0.5
+            )
+
+        q_grouped = []
+        for j in range(PACK):
+            grouped = stage.tile([P, P, PACK], BF16, align_bytes=64)
+            q_grouped.append(grouped)
+            transpose_tile(q_sb[:, j, :], grouped[:])
+
+        step_planes = keep.tile([P, PACK, P], F32)
+        mnew_planes = keep.tile([P, PACK, P], F32)
+        mnew_grouped = keep.tile([P, P, PACK], BF16, align_bytes=64)
+        mnew_codes = keep.tile([P, P], U32, align_bytes=64)
+        mnew_scales = keep.tile([P, P], U8, align_bytes=64)
+
+        def take_step(u):
+            ts = slice(2 * u, 2 * u + 2)
+            nc.vector.scalar_tensor_tensor(
+                out=step_planes[:, ts, :],
+                in0=tanh_planes[:, ts, :],
+                scalar=1.0,
+                in1=diff_planes[:, ts, :],
+                op0=ALU.add,
+                op1=ALU.mult,
+            )
+
+        def blend(u):
+            ts = slice(2 * u, 2 * u + 2)
+            nc.vector.scalar_tensor_tensor(
+                out=mnew_planes[:, ts, :],
+                in0=step_planes[:, ts, :],
+                scalar=0.5,
+                in1=mem_planes[:, ts, :],
+                op0=ALU.mult,
+                op1=ALU.add,
+            )
+
+        def round_and_group(u):
+            ts = slice(2 * u, 2 * u + 2)
+            nc.vector.tensor_copy(
+                out=mnew_grouped[:, :, ts], in_=mnew_planes[:, ts, :].rearrange("p e m -> p m e")
+            )
+
+        def quantise_queries(j):
+            chunk = slice(j * P, (j + 1) * P)
+            quantise(q_grouped[j][:], q_codes[:, chunk], q_scales[:, chunk])
+
+        take_step(0)
+        blend(0)
+        take_step(1)
+        round_and_group(0)
+        blend(1)
+        quantise_queries(0)
+        round_and_group(1)
+        quantise_queries(1)
+        quantise(mnew_grouped[:], mnew_codes[:], mnew_scales[:])
+        quantise_queries(2)
+        quantise_queries(3)
+
+        back_ps = back_psum.tile([P, PACK, P], F32)
+        for t in range(PACK):
+            nc.tensor.transpose(back_ps[:, t, :], mnew_planes[:, t, :], identity[:])
+        mnew_out = keep.tile([P, D], F32)
+        nc.scalar.copy(
+            out=mnew_out[:].rearrange("m (p t) -> m p t", t=PACK),
+            in_=back_ps[:].rearrange("m t p -> m p t"),
+        )
+        nc.sync.dma_start(out=out_0, in_=mnew_out[:])
+
+        logit_halves = []
+        for h in range(2):
+            logit_ps = half_psum.tile([P, 2, P], F32, tag="half")
+            logit_halves.append(logit_ps)
+            for i in range(2):
+                chunk = slice((2 * h + i) * P, (2 * h + i + 1) * P)
+                nc.tensor.matmul_mx(
+                    out=logit_ps[:, i, :],
+                    lhsT=q_codes[:, chunk].bitcast(FP8X4),
+                    lhsT_scale=q_scales[:, chunk],
+                    rhs=mnew_codes[:].bitcast(FP8X4),
+                    rhs_scale=mnew_scales[:],
+                    start=True,
+                    stop=True,
+                )
+
+        negated = keep.tile([P, PACK, P], F32)
+        shift = keep.tile([P, PACK], F32)
+        expd = keep.tile([P, PACK, P], F32)
+        sums = keep.tile([P, PACK], F32)
+        inv_sums = keep.tile([P, PACK], F32)
+        w_att = keep.tile([P, PACK, P], F32)
+        for j in range(PACK):
+            nc.vector.tensor_scalar(
+                out=negated[:, j, :],
+                in0=logit_halves[j // 2][:, j % 2, :],
+                scalar1=-INV_TEMP,
+                scalar2=None,
+                op0=ALU.mult,
+                op1=ALU.min,
+                accum_out=shift[:, j : j + 1],
+            )
+            nc.scalar.activation(
+                out=expd[:, j, :],
+                in_=negated[:, j, :],
+                func=ACT.Exp,
+                bias=shift[:, j : j + 1],
+                scale=-1.0,
+                accum_out=sums[:, j : j + 1],
+            )
+        out_rows = out_1.rearrange("t b m -> (t b) m").rearrange("(r j) m -> r j m", j=PACK)
+        for h in range(2):
+            js = slice(2 * h, 2 * h + 2)
+            nc.vector.reciprocal(out=inv_sums[:, js], in_=sums[:, js])
+            for j in (2 * h, 2 * h + 1):
+                nc.vector.tensor_scalar_mul(
+                    out=w_att[:, j, :], in0=expd[:, j, :], scalar1=inv_sums[:, j : j + 1]
+                )
+            nc.sync.dma_start(out=out_rows[:, js, :], in_=w_att[:, js, :])

@@ -27,9 +27,9 @@ def tile_gatedmemorymodule_pb_s_kernel(
     with ExitStack() as ctx:
         ctx.enter_context(tc.manual_schedule())
         keep = ctx.enter_context(tc.tile_pool(name="keep", bufs=1))
-        stage = ctx.enter_context(tc.tile_pool(name="stage", bufs=4))
+        stage = ctx.enter_context(tc.tile_pool(name="stage", bufs=12))
         flip_psum = ctx.enter_context(tc.psum_pool(name="flip_psum", bufs=4))
-        half_psum = ctx.enter_context(tc.psum_pool(name="half_psum", bufs=2))
+        half_psum = ctx.enter_context(tc.psum_pool(name="half_psum", bufs=1))
         back_psum = ctx.enter_context(tc.psum_pool(name="back_psum", bufs=1))
 
         identity = keep.tile([P, P], F32)
@@ -39,6 +39,12 @@ def tile_gatedmemorymodule_pb_s_kernel(
         nc.vector.memset(zero[:], 0.0)
         warm = keep.tile([P, 1], F32)
         nc.scalar.activation(out=warm[:], in_=zero[:], func=ACT.Exp)
+
+        zeros = keep.tile([P, P], F32)
+        nc.vector.memset(zeros[:], 0.0)
+        idle_ps = back_psum.tile([P, PACK, P], F32, tag="back", name="idle_ps")
+        for t in range(2):
+            nc.tensor.matmul(idle_ps[:, t, :], lhsT=zeros[:], rhs=zeros[:], start=True, stop=True)
 
         slots_sb = keep.tile([P, 2, D], BF16)
         nc.sync.dma_start(out=slots_sb[:, 0, :], in_=memory_items)
@@ -57,12 +63,12 @@ def tile_gatedmemorymodule_pb_s_kernel(
             js = slice(2 * h, 2 * h + 2)
             nc.sync.dma_start(out=q_sb[:, js, :].rearrange("r i d -> r (i d)"), in_=q_rows[h])
 
-        def transpose_tile(rows_sb, grouped):
+        def transpose_tile(rows_sb, grouped, copy=nc.scalar.copy):
             words = rows_sb.bitcast(F32)
             flipped = flip_psum.tile([P, 2, P], F32)
             for u in range(2):
                 nc.tensor.transpose(flipped[:, u, :], words[:, u : 2 * P : 2], identity[:])
-            nc.scalar.copy(
+            copy(
                 out=grouped.rearrange("p r t -> p (r t)").bitcast(F32).rearrange("p (r u) -> p r u", u=2),
                 in_=flipped[:].rearrange("p u r -> p r u"),
             )
@@ -81,74 +87,93 @@ def tile_gatedmemorymodule_pb_s_kernel(
         q_codes = keep.tile([P, PACK * P], U32, align_bytes=64)
         q_scales = keep.tile([P, PACK * P], U8, align_bytes=64)
 
+        diff_rows = keep.tile([P, D], F32)
+        nc.vector.tensor_tensor(
+            out=diff_rows[:], in0=slots_sb[:, 1, :], in1=slots_sb[:, 0, :], op=ALU.subtract
+        )
+
         slots_grouped = keep.tile([P, 2, P, PACK], BF16, align_bytes=64)
         for i in range(2):
-            chunk = slice(i * P, (i + 1) * P)
             transpose_tile(slots_sb[:, i, :], slots_grouped[:, i, :, :])
-            quantise(slots_grouped[:, i, :, :], slot_codes[:, chunk], slot_scales[:, chunk])
-        mem_planes = slots_grouped[:, 0, :, :].rearrange("p m t -> p t m")
-        wq_planes = slots_grouped[:, 1, :, :].rearrange("p m t -> p t m")
-        diff_planes = keep.tile([P, PACK, P], F32)
-        nc.vector.tensor_tensor(out=diff_planes[:], in0=wq_planes, in1=mem_planes, op=ALU.subtract)
+        quantise(slots_grouped[:].rearrange("p i r t -> p (i r) t"), slot_codes[:], slot_scales[:])
 
-        for u in range(2):
-            for rows, codes, scales in ((u_sb, u_codes, u_scales), (w_sb, w_codes, w_scales)):
-                for t in (2 * u, 2 * u + 1):
-                    chunk = slice(t * P, (t + 1) * P)
-                    grouped = stage.tile([P, P, PACK], BF16, align_bytes=64)
-                    transpose_tile(rows[:, t, :], grouped[:])
-                    quantise(grouped[:], codes[:, chunk], scales[:, chunk])
+        u_pair = keep.tile([P, 2, P, PACK], BF16, align_bytes=64)
+        w_pair = keep.tile([P, 2, P, PACK], BF16, align_bytes=64)
+        pair = slice(0, 2 * P)
+        transpose_tile(u_sb[:, 0, :], u_pair[:, 0, :, :])
+        transpose_tile(u_sb[:, 1, :], u_pair[:, 1, :, :])
+        transpose_tile(w_sb[:, 0, :], w_pair[:, 0, :, :], nc.vector.tensor_copy)
+        transpose_tile(w_sb[:, 1, :], w_pair[:, 1, :, :])
+        quantise(u_pair[:].rearrange("p i r t -> p (i r) t"), u_codes[:, pair], u_scales[:, pair])
+        quantise(w_pair[:].rearrange("p i r t -> p (i r) t"), w_codes[:, pair], w_scales[:, pair])
 
-        gate_halves = []
-        for u in range(2):
-            gate_ps = half_psum.tile([P, 2, P], F32, tag="half")
-            gate_halves.append(gate_ps)
-            for e in range(2):
-                chunk = slice((2 * u + e) * P, (2 * u + e + 1) * P)
-                nc.tensor.matmul_mx(
-                    out=gate_ps[:, e, :],
-                    lhsT=u_codes[:, chunk].bitcast(FP8X4),
-                    lhsT_scale=u_scales[:, chunk],
-                    rhs=slot_codes[:, 0:P].bitcast(FP8X4),
-                    rhs_scale=slot_scales[:, 0:P],
-                    start=True,
-                    stop=False,
-                )
-                nc.tensor.matmul_mx(
-                    out=gate_ps[:, e, :],
-                    lhsT=w_codes[:, chunk].bitcast(FP8X4),
-                    lhsT_scale=w_scales[:, chunk],
-                    rhs=slot_codes[:, P : 2 * P].bitcast(FP8X4),
-                    rhs_scale=slot_scales[:, P : 2 * P],
-                    start=False,
-                    stop=True,
-                )
+        diff_ps = back_psum.tile([P, PACK, P], F32, tag="back", name="diff_ps")
+        for t in range(PACK):
+            nc.tensor.transpose(diff_ps[:, t, :], diff_rows[:, t : D : PACK], identity[:])
 
-        tanh_planes = keep.tile([P, PACK, P], F32)
-        for u in range(2):
-            nc.scalar.activation(
-                out=tanh_planes[:, 2 * u : 2 * u + 2, :], in_=gate_halves[u][:], func=ACT.Tanh, scale=0.5
+        for rows, codes, scales in ((u_sb, u_codes, u_scales), (w_sb, w_codes, w_scales)):
+            for t in (2, 3):
+                chunk = slice(t * P, (t + 1) * P)
+                grouped = stage.tile([P, P, PACK], BF16, align_bytes=64)
+                transpose_tile(rows[:, t, :], grouped[:])
+                quantise(grouped[:], codes[:, chunk], scales[:, chunk])
+
+        def gate_passes(gate_ps, i, t):
+            chunk = slice(t * P, (t + 1) * P)
+            nc.tensor.matmul_mx(
+                out=gate_ps[:, i, :],
+                lhsT=u_codes[:, chunk].bitcast(FP8X4),
+                lhsT_scale=u_scales[:, chunk],
+                rhs=slot_codes[:, 0:P].bitcast(FP8X4),
+                rhs_scale=slot_scales[:, 0:P],
+                start=True,
+                stop=False,
+            )
+            nc.tensor.matmul_mx(
+                out=gate_ps[:, i, :],
+                lhsT=w_codes[:, chunk].bitcast(FP8X4),
+                lhsT_scale=w_scales[:, chunk],
+                rhs=slot_codes[:, P : 2 * P].bitcast(FP8X4),
+                rhs_scale=slot_scales[:, P : 2 * P],
+                start=False,
+                stop=True,
             )
 
-        q_grouped = []
-        for j in range(PACK):
-            grouped = stage.tile([P, P, PACK], BF16, align_bytes=64)
-            q_grouped.append(grouped)
-            transpose_tile(q_sb[:, j, :], grouped[:])
-
+        tanh_planes = keep.tile([P, PACK, P], F32)
         step_planes = keep.tile([P, PACK, P], F32)
-        mnew_planes = keep.tile([P, PACK, P], F32)
+        q_grouped = [stage.tile([P, P, PACK], BF16, align_bytes=64, name="q_grouped") for j in range(PACK)]
+        gates = [half_psum.tile([P, 2, P], F32, tag=name, name="gate_" + name) for name in "abc"]
+
+        def take_tanh(gate_ps, first, last):
+            nc.scalar.activation(
+                out=tanh_planes[:, first : last + 1, :],
+                in_=gate_ps[:, 0 : last - first + 1, :],
+                func=ACT.Tanh,
+                scale=0.5,
+            )
+
+        gate_passes(gates[0], 0, 0)
+        gate_passes(gates[0], 1, 1)
+        take_tanh(gates[0], 0, 1)
+        gate_passes(gates[1], 0, 2)
+        take_tanh(gates[1], 2, 2)
+        gate_passes(gates[2], 0, 3)
+        take_tanh(gates[2], 3, 3)
+
+        for j in range(PACK):
+            transpose_tile(q_sb[:, j, :], q_grouped[j][:])
+
         mnew_grouped = keep.tile([P, P, PACK], BF16, align_bytes=64)
         mnew_codes = keep.tile([P, P], U32, align_bytes=64)
         mnew_scales = keep.tile([P, P], U8, align_bytes=64)
 
-        def take_step(u):
-            ts = slice(2 * u, 2 * u + 2)
+        def take_step(first, last):
+            ts = slice(first, last + 1)
             nc.vector.scalar_tensor_tensor(
                 out=step_planes[:, ts, :],
                 in0=tanh_planes[:, ts, :],
                 scalar=1.0,
-                in1=diff_planes[:, ts, :],
+                in1=diff_ps[:, ts, :],
                 op0=ALU.add,
                 op1=ALU.mult,
             )
@@ -156,49 +181,46 @@ def tile_gatedmemorymodule_pb_s_kernel(
         def blend(u):
             ts = slice(2 * u, 2 * u + 2)
             nc.vector.scalar_tensor_tensor(
-                out=mnew_planes[:, ts, :],
-                in0=step_planes[:, ts, :],
+                out=mnew_grouped[:, :, ts],
+                in0=step_planes[:, ts, :].rearrange("p e m -> p m e"),
                 scalar=0.5,
-                in1=mem_planes[:, ts, :],
+                in1=slots_grouped[:, 0, :, ts],
                 op0=ALU.mult,
                 op1=ALU.add,
-            )
-
-        def round_and_group(u):
-            ts = slice(2 * u, 2 * u + 2)
-            nc.vector.tensor_copy(
-                out=mnew_grouped[:, :, ts], in_=mnew_planes[:, ts, :].rearrange("p e m -> p m e")
             )
 
         def quantise_queries(j):
             chunk = slice(j * P, (j + 1) * P)
             quantise(q_grouped[j][:], q_codes[:, chunk], q_scales[:, chunk])
 
-        take_step(0)
-        blend(0)
-        take_step(1)
-        round_and_group(0)
-        blend(1)
+        take_step(0, 1)
+        take_step(2, 2)
+        take_step(3, 3)
         quantise_queries(0)
-        round_and_group(1)
+        blend(0)
+        blend(1)
         quantise_queries(1)
         quantise(mnew_grouped[:], mnew_codes[:], mnew_scales[:])
         quantise_queries(2)
         quantise_queries(3)
 
-        back_ps = back_psum.tile([P, PACK, P], F32)
+        back_ps = back_psum.tile([P, PACK, P], F32, tag="back", name="back_ps")
         for t in range(PACK):
-            nc.tensor.transpose(back_ps[:, t, :], mnew_planes[:, t, :], identity[:])
-        mnew_out = keep.tile([P, D], F32)
-        nc.scalar.copy(
-            out=mnew_out[:].rearrange("m (p t) -> m p t", t=PACK),
+            nc.tensor.transpose(back_ps[:, t, :], step_planes[:, t, :], identity[:])
+        half_step = keep.tile([P, D], F32)
+        nc.scalar.activation(
+            out=half_step[:].rearrange("m (p t) -> m p t", t=PACK),
             in_=back_ps[:].rearrange("m t p -> m p t"),
+            func=ACT.Copy,
+            scale=0.5,
         )
+        mnew_out = keep.tile([P, D], F32)
+        nc.gpsimd.tensor_tensor(out=mnew_out[:], in0=half_step[:], in1=slots_sb[:, 0, :], op=ALU.add)
         nc.sync.dma_start(out=out_0, in_=mnew_out[:])
 
         logit_halves = []
-        for h in range(2):
-            logit_ps = half_psum.tile([P, 2, P], F32, tag="half")
+        for h, name in enumerate(("a", "b")):
+            logit_ps = half_psum.tile([P, 2, P], F32, tag=name, name="logits_" + name)
             logit_halves.append(logit_ps)
             for i in range(2):
                 chunk = slice((2 * h + i) * P, (2 * h + i + 1) * P)

@@ -53,10 +53,12 @@ def tile_gatedmemorymodule_pb_s_kernel(
         w_rows = W_w.rearrange("(p u e) d -> u p (e d)", u=2, e=2)
         u_sb = keep.tile([P, PACK, D], BF16)
         w_sb = keep.tile([P, PACK, D], BF16)
-        for u in range(2):
+        for sb, rows, u in ((u_sb, u_rows, 0), (w_sb, w_rows, 0), (u_sb, u_rows, 1)):
             ts = slice(2 * u, 2 * u + 2)
-            nc.sync.dma_start(out=u_sb[:, ts, :].rearrange("p e d -> p (e d)"), in_=u_rows[u])
-            nc.sync.dma_start(out=w_sb[:, ts, :].rearrange("p e d -> p (e d)"), in_=w_rows[u])
+            nc.sync.dma_start(out=sb[:, ts, :].rearrange("p e d -> p (e d)"), in_=rows[u])
+        w_tiles = W_w.rearrange("(p t) d -> t p d", t=PACK)
+        for t in (2, 3):
+            nc.sync.dma_start(out=w_sb[:, t, :], in_=w_tiles[t])
         q_rows = queries.rearrange("t b d -> (t b) d").rearrange("(r h i) d -> h r (i d)", h=2, i=2)
         q_sb = keep.tile([P, PACK, D], BF16)
         for h in range(2):
@@ -87,9 +89,12 @@ def tile_gatedmemorymodule_pb_s_kernel(
         q_codes = keep.tile([P, PACK * P], U32, align_bytes=64)
         q_scales = keep.tile([P, PACK * P], U8, align_bytes=64)
 
-        diff_rows = keep.tile([P, D], F32)
+        diff_rows = keep.tile([P, PACK, P], F32)
         nc.vector.tensor_tensor(
-            out=diff_rows[:], in0=slots_sb[:, 1, :], in1=slots_sb[:, 0, :], op=ALU.subtract
+            out=diff_rows[:],
+            in0=slots_sb[:, 1, :].rearrange("m (p t) -> m t p", t=PACK),
+            in1=slots_sb[:, 0, :].rearrange("m (p t) -> m t p", t=PACK),
+            op=ALU.subtract,
         )
 
         slots_grouped = keep.tile([P, 2, P, PACK], BF16, align_bytes=64)
@@ -97,26 +102,31 @@ def tile_gatedmemorymodule_pb_s_kernel(
             transpose_tile(slots_sb[:, i, :], slots_grouped[:, i, :, :])
         quantise(slots_grouped[:].rearrange("p i r t -> p (i r) t"), slot_codes[:], slot_scales[:])
 
-        u_pair = keep.tile([P, 2, P, PACK], BF16, align_bytes=64)
-        w_pair = keep.tile([P, 2, P, PACK], BF16, align_bytes=64)
-        pair = slice(0, 2 * P)
-        transpose_tile(u_sb[:, 0, :], u_pair[:, 0, :, :])
-        transpose_tile(u_sb[:, 1, :], u_pair[:, 1, :, :])
-        transpose_tile(w_sb[:, 0, :], w_pair[:, 0, :, :], nc.vector.tensor_copy)
-        transpose_tile(w_sb[:, 1, :], w_pair[:, 1, :, :])
-        quantise(u_pair[:].rearrange("p i r t -> p (i r) t"), u_codes[:, pair], u_scales[:, pair])
-        quantise(w_pair[:].rearrange("p i r t -> p (i r) t"), w_codes[:, pair], w_scales[:, pair])
+        u_pairs = [keep.tile([P, 2, P, PACK], BF16, align_bytes=64, name="u_pair%d" % u) for u in range(2)]
+        w_pairs = [keep.tile([P, 2, P, PACK], BF16, align_bytes=64, name="w_pair%d" % u) for u in range(2)]
+
+        def quantise_pair(pairs, codes, scales, u):
+            pair = slice(2 * u * P, (2 * u + 2) * P)
+            quantise(pairs[u][:].rearrange("p i r t -> p (i r) t"), codes[:, pair], scales[:, pair])
+
+        transpose_tile(u_sb[:, 0, :], u_pairs[0][:, 0, :, :])
+        transpose_tile(u_sb[:, 1, :], u_pairs[0][:, 1, :, :])
+        transpose_tile(w_sb[:, 0, :], w_pairs[0][:, 0, :, :], nc.vector.tensor_copy)
+        transpose_tile(w_sb[:, 1, :], w_pairs[0][:, 1, :, :])
+        quantise_pair(u_pairs, u_codes, u_scales, 0)
+        transpose_tile(u_sb[:, 2, :], u_pairs[1][:, 0, :, :])
+        transpose_tile(u_sb[:, 3, :], u_pairs[1][:, 1, :, :], nc.vector.tensor_copy)
+        quantise_pair(w_pairs, w_codes, w_scales, 0)
+        quantise_pair(u_pairs, u_codes, u_scales, 1)
+        for t in (2, 3):
+            chunk = slice(t * P, (t + 1) * P)
+            grouped = w_pairs[1][:, t - 2, :, :]
+            transpose_tile(w_sb[:, t, :], grouped)
+            quantise(grouped, w_codes[:, chunk], w_scales[:, chunk])
 
         diff_ps = back_psum.tile([P, PACK, P], F32, tag="back", name="diff_ps")
         for t in range(PACK):
-            nc.tensor.transpose(diff_ps[:, t, :], diff_rows[:, t : D : PACK], identity[:])
-
-        for rows, codes, scales in ((u_sb, u_codes, u_scales), (w_sb, w_codes, w_scales)):
-            for t in (2, 3):
-                chunk = slice(t * P, (t + 1) * P)
-                grouped = stage.tile([P, P, PACK], BF16, align_bytes=64)
-                transpose_tile(rows[:, t, :], grouped[:])
-                quantise(grouped[:], codes[:, chunk], scales[:, chunk])
+            nc.tensor.transpose(diff_ps[:, t, :], diff_rows[:, t, :], identity[:])
 
         def gate_passes(gate_ps, i, t):
             chunk = slice(t * P, (t + 1) * P)
@@ -152,17 +162,6 @@ def tile_gatedmemorymodule_pb_s_kernel(
                 scale=0.5,
             )
 
-        gate_passes(gates[0], 0, 0)
-        gate_passes(gates[0], 1, 1)
-        take_tanh(gates[0], 0, 1)
-        gate_passes(gates[1], 0, 2)
-        take_tanh(gates[1], 2, 2)
-        gate_passes(gates[2], 0, 3)
-        take_tanh(gates[2], 3, 3)
-
-        for j in range(PACK):
-            transpose_tile(q_sb[:, j, :], q_grouped[j][:])
-
         mnew_grouped = keep.tile([P, P, PACK], BF16, align_bytes=64)
         mnew_codes = keep.tile([P, P], U32, align_bytes=64)
         mnew_scales = keep.tile([P, P], U8, align_bytes=64)
@@ -193,10 +192,20 @@ def tile_gatedmemorymodule_pb_s_kernel(
             chunk = slice(j * P, (j + 1) * P)
             quantise(q_grouped[j][:], q_codes[:, chunk], q_scales[:, chunk])
 
+        transpose_tile(q_sb[:, 0, :], q_grouped[0][:])
+        quantise_queries(0)
+        gate_passes(gates[0], 0, 0)
+        gate_passes(gates[0], 1, 1)
+        take_tanh(gates[0], 0, 1)
+        gate_passes(gates[1], 0, 2)
+        take_tanh(gates[1], 2, 2)
+        gate_passes(gates[2], 0, 3)
+        take_tanh(gates[2], 3, 3)
+        for j in range(1, PACK):
+            transpose_tile(q_sb[:, j, :], q_grouped[j][:])
         take_step(0, 1)
         take_step(2, 2)
         take_step(3, 3)
-        quantise_queries(0)
         blend(0)
         blend(1)
         quantise_queries(1)
@@ -208,15 +217,20 @@ def tile_gatedmemorymodule_pb_s_kernel(
         for t in range(PACK):
             nc.tensor.transpose(back_ps[:, t, :], step_planes[:, t, :], identity[:])
         half_step = keep.tile([P, D], F32)
-        nc.scalar.activation(
-            out=half_step[:].rearrange("m (p t) -> m p t", t=PACK),
-            in_=back_ps[:].rearrange("m t p -> m p t"),
-            func=ACT.Copy,
-            scale=0.5,
-        )
         mnew_out = keep.tile([P, D], F32)
-        nc.gpsimd.tensor_tensor(out=mnew_out[:], in0=half_step[:], in1=slots_sb[:, 0, :], op=ALU.add)
-        nc.sync.dma_start(out=out_0, in_=mnew_out[:])
+        for h in range(2):
+            ps = slice(h * P // 2, (h + 1) * P // 2)
+            ds = slice(h * D // 2, (h + 1) * D // 2)
+            nc.scalar.activation(
+                out=half_step[:, ds].rearrange("m (p t) -> m p t", t=PACK),
+                in_=back_ps[:, :, ps].rearrange("m t p -> m p t"),
+                func=ACT.Copy,
+                scale=0.5,
+            )
+            nc.gpsimd.tensor_tensor(
+                out=mnew_out[:, ds], in0=half_step[:, ds], in1=slots_sb[:, 0, ds], op=ALU.add
+            )
+            nc.sync.dma_start(out=out_0[:, ds], in_=mnew_out[:, ds])
 
         logit_halves = []
         for h, name in enumerate(("a", "b")):
@@ -259,11 +273,18 @@ def tile_gatedmemorymodule_pb_s_kernel(
                 accum_out=sums[:, j : j + 1],
             )
         out_rows = out_1.rearrange("t b m -> (t b) m").rearrange("(r j) m -> r j m", j=PACK)
-        for h in range(2):
-            js = slice(2 * h, 2 * h + 2)
-            nc.vector.reciprocal(out=inv_sums[:, js], in_=sums[:, js])
-            for j in (2 * h, 2 * h + 1):
-                nc.vector.tensor_scalar_mul(
-                    out=w_att[:, j, :], in0=expd[:, j, :], scalar1=inv_sums[:, j : j + 1]
-                )
-            nc.sync.dma_start(out=out_rows[:, js, :], in_=w_att[:, js, :])
+
+        def invert(j):
+            nc.vector.reciprocal(out=inv_sums[:, j : j + 1], in_=sums[:, j : j + 1])
+
+        def normalise(j):
+            nc.vector.tensor_scalar_mul(out=w_att[:, j, :], in0=expd[:, j, :], scalar1=inv_sums[:, j : j + 1])
+
+        invert(0)
+        for j in range(PACK):
+            if j + 1 < PACK:
+                invert(j + 1)
+            normalise(j)
+            if j % 2 == 1:
+                js = slice(j - 1, j + 1)
+                nc.sync.dma_start(out=out_rows[:, js, :], in_=w_att[:, js, :])

@@ -40,11 +40,10 @@ def tile_gatedmemorymodule_pb_s_kernel(
         warm = keep.tile([P, 1], F32)
         nc.scalar.activation(out=warm[:], in_=zero[:], func=ACT.Exp)
 
-        zeros = keep.tile([P, P], F32)
-        nc.vector.memset(zeros[:], 0.0)
+        zeros = zero[:].to_broadcast([P, P])
         idle_ps = back_psum.tile([P, PACK, P], F32, tag="back", name="idle_ps")
-        for t in range(2):
-            nc.tensor.matmul(idle_ps[:, t, :], lhsT=zeros[:], rhs=zeros[:], start=True, stop=True)
+        for t in range(PACK):
+            nc.tensor.matmul(idle_ps[:, t, :], lhsT=zeros, rhs=zeros, start=True, stop=True)
 
         slots_sb = keep.tile([P, 2, D], BF16)
         nc.sync.dma_start(out=slots_sb[:, 0, :], in_=memory_items)

@@ -40,10 +40,19 @@ def tile_gatedmemorymodule_pb_s_kernel(
         warm = keep.tile([P, 1], F32)
         nc.scalar.activation(out=warm[:], in_=zero[:], func=ACT.Exp)
 
-        zeros = zero[:].to_broadcast([P, P])
         idle_ps = back_psum.tile([P, PACK, P], F32, tag="back", name="idle_ps")
-        for t in range(PACK):
-            nc.tensor.matmul(idle_ps[:, t, :], lhsT=zeros, rhs=zeros, start=True, stop=True)
+
+        def fill_time(columns):
+            nc.tensor.matmul(
+                idle_ps[:, 0, 0:columns],
+                lhsT=zero[:].to_broadcast([P, P]),
+                rhs=zero[:].to_broadcast([P, columns]),
+                start=True,
+                stop=True,
+            )
+
+        for step in range(3):
+            fill_time(P)
 
         slots_sb = keep.tile([P, 2, D], BF16)
         nc.sync.dma_start(out=slots_sb[:, 0, :], in_=memory_items)
@@ -99,6 +108,7 @@ def tile_gatedmemorymodule_pb_s_kernel(
         slots_grouped = keep.tile([P, 2, P, PACK], BF16, align_bytes=64)
         for i in range(2):
             transpose_tile(slots_sb[:, i, :], slots_grouped[:, i, :, :])
+        fill_time(P)
         quantise(slots_grouped[:].rearrange("p i r t -> p (i r) t"), slot_codes[:], slot_scales[:])
 
         u_pairs = [keep.tile([P, 2, P, PACK], BF16, align_bytes=64, name="u_pair%d" % u) for u in range(2)]
@@ -112,6 +122,7 @@ def tile_gatedmemorymodule_pb_s_kernel(
         transpose_tile(u_sb[:, 1, :], u_pairs[0][:, 1, :, :])
         transpose_tile(w_sb[:, 0, :], w_pairs[0][:, 0, :, :], nc.vector.tensor_copy)
         transpose_tile(w_sb[:, 1, :], w_pairs[0][:, 1, :, :])
+        fill_time(96)
         quantise_pair(u_pairs, u_codes, u_scales, 0)
         transpose_tile(u_sb[:, 2, :], u_pairs[1][:, 0, :, :])
         transpose_tile(u_sb[:, 3, :], u_pairs[1][:, 1, :, :], nc.vector.tensor_copy)

@@ -125,7 +125,7 @@ def tile_gatedmemorymodule_pb_s_kernel(
         fill_time(96)
         quantise_pair(u_pairs, u_codes, u_scales, 0)
         transpose_tile(u_sb[:, 2, :], u_pairs[1][:, 0, :, :])
-        transpose_tile(u_sb[:, 3, :], u_pairs[1][:, 1, :, :], nc.vector.tensor_copy)
+        transpose_tile(u_sb[:, 3, :], u_pairs[1][:, 1, :, :])
         quantise_pair(w_pairs, w_codes, w_scales, 0)
         quantise_pair(u_pairs, u_codes, u_scales, 1)
         for t in (2, 3):
@@ -202,8 +202,6 @@ def tile_gatedmemorymodule_pb_s_kernel(
             chunk = slice(j * P, (j + 1) * P)
             quantise(q_grouped[j][:], q_codes[:, chunk], q_scales[:, chunk])
 
-        transpose_tile(q_sb[:, 0, :], q_grouped[0][:])
-        quantise_queries(0)
         gate_passes(gates[0], 0, 0)
         gate_passes(gates[0], 1, 1)
         take_tanh(gates[0], 0, 1)
@@ -211,17 +209,17 @@ def tile_gatedmemorymodule_pb_s_kernel(
         take_tanh(gates[1], 2, 2)
         gate_passes(gates[2], 0, 3)
         take_tanh(gates[2], 3, 3)
-        for j in range(1, PACK):
+        for j in range(PACK):
             transpose_tile(q_sb[:, j, :], q_grouped[j][:])
         take_step(0, 1)
         take_step(2, 2)
         take_step(3, 3)
         blend(0)
         blend(1)
-        quantise_queries(1)
+        quantise_queries(0)
         quantise(mnew_grouped[:], mnew_codes[:], mnew_scales[:])
-        quantise_queries(2)
-        quantise_queries(3)
+        for j in range(1, PACK):
+            quantise_queries(j)
 
         back_ps = back_psum.tile([P, PACK, P], F32, tag="back", name="back_ps")
         for t in range(PACK):

@@ -61,12 +61,10 @@ def tile_gatedmemorymodule_pb_s_kernel(
         w_rows = W_w.rearrange("(p u e) d -> u p (e d)", u=2, e=2)
         u_sb = keep.tile([P, PACK, D], BF16)
         w_sb = keep.tile([P, PACK, D], BF16)
-        for sb, rows, u in ((u_sb, u_rows, 0), (w_sb, w_rows, 0), (u_sb, u_rows, 1)):
+        for u in range(2):
             ts = slice(2 * u, 2 * u + 2)
-            nc.sync.dma_start(out=sb[:, ts, :].rearrange("p e d -> p (e d)"), in_=rows[u])
-        w_tiles = W_w.rearrange("(p t) d -> t p d", t=PACK)
-        for t in (2, 3):
-            nc.sync.dma_start(out=w_sb[:, t, :], in_=w_tiles[t])
+            nc.sync.dma_start(out=u_sb[:, ts, :].rearrange("p e d -> p (e d)"), in_=u_rows[u])
+            nc.sync.dma_start(out=w_sb[:, ts, :].rearrange("p e d -> p (e d)"), in_=w_rows[u])
         q_rows = queries.rearrange("t b d -> (t b) d").rearrange("(r h i) d -> h r (i d)", h=2, i=2)
         q_sb = keep.tile([P, PACK, D], BF16)
         for h in range(2):

from contextlib import ExitStack

import concourse.mybir as mybir
from concourse.masks import make_identity

F32 = mybir.dt.float32
BF16 = mybir.dt.bfloat16
U32 = mybir.dt.uint32
U8 = mybir.dt.uint8
FP8X4 = mybir.dt.float8_e4m3fn_x4
ACT = mybir.ActivationFunctionType
ALU = mybir.AluOpType
AXIS = mybir.AxisListType

P = 128
D = 512
PACK = 4
INV_TEMP = 10.0

FLOPS = 2 * (2 * P * D * D) + 2 * (4 * P) * D * P


def tile_gatedmemorymodule_pb_s_kernel(
    tc, queries, memory_items, wq, U_w, W_w, out_0, out_1
):
    nc = tc.nc
    with ExitStack() as ctx:
        ctx.enter_context(tc.manual_schedule())
        keep = ctx.enter_context(tc.tile_pool(name="keep", bufs=1))
        stage = ctx.enter_context(tc.tile_pool(name="stage", bufs=12))
        flip_psum = ctx.enter_context(tc.psum_pool(name="flip_psum", bufs=4))
        half_psum = ctx.enter_context(tc.psum_pool(name="half_psum", bufs=1))
        back_psum = ctx.enter_context(tc.psum_pool(name="back_psum", bufs=1))

        identity = keep.tile([P, P], F32)
        make_identity(nc, identity[:])

        zero = keep.tile([P, 1], F32)
        nc.vector.memset(zero[:], 0.0)
        warm = keep.tile([P, 1], F32)
        nc.scalar.activation(out=warm[:], in_=zero[:], func=ACT.Exp)

        idle_ps = back_psum.tile([P, PACK, P], F32, tag="back", name="idle_ps")

        def fill_time(columns):
            nc.tensor.matmul(
                idle_ps[:, 0, 0:columns],
                lhsT=zero[:].to_broadcast([P, P]),
                rhs=zero[:].to_broadcast([P, columns]),
                start=True,
                stop=True,
            )

        for step in range(3):
            fill_time(P)

        slots_sb = keep.tile([P, 2, D], BF16)
        nc.sync.dma_start(out=slots_sb[:, 0, :], in_=memory_items)
        nc.sync.dma_start(out=slots_sb[:, 1, :], in_=wq)
        u_rows = U_w.rearrange("(p u e) d -> u p (e d)", u=2, e=2)
        w_rows = W_w.rearrange("(p u e) d -> u p (e d)", u=2, e=2)
        u_sb = keep.tile([P, PACK, D], BF16)
        w_sb = keep.tile([P, PACK, D], BF16)
        for u in range(2):
            ts = slice(2 * u, 2 * u + 2)
            nc.sync.dma_start(out=u_sb[:, ts, :].rearrange("p e d -> p (e d)"), in_=u_rows[u])
            nc.sync.dma_start(out=w_sb[:, ts, :].rearrange("p e d -> p (e d)"), in_=w_rows[u])
        q_rows = queries.rearrange("t b d -> (t b) d").rearrange("(r h i) d -> h r (i d)", h=2, i=2)
        q_sb = keep.tile([P, PACK, D], BF16)
        for h in range(2):
            js = slice(2 * h, 2 * h + 2)
            nc.sync.dma_start(out=q_sb[:, js, :].rearrange("r i d -> r (i d)"), in_=q_rows[h])

        def transpose_tile(rows_sb, grouped, copy=nc.scalar.copy):
            words = rows_sb.bitcast(F32)
            flipped = flip_psum.tile([P, 2, P], F32)
            for u in range(2):
                nc.tensor.transpose(flipped[:, u, :], words[:, u : 2 * P : 2], identity[:])
            copy(
                out=grouped.rearrange("p r t -> p (r t)").bitcast(F32).rearrange("p (r u) -> p r u", u=2),
                in_=flipped[:].rearrange("p u r -> p r u"),
            )

        def quantise(grouped, codes, scales):
            nc.vector.quantize_mx(
                out=codes.bitcast(FP8X4), scales=scales, in_=grouped.rearrange("p r t -> p (r t)")
            )

        slot_codes = keep.tile([P, 2 * P], U32, align_bytes=64)
        slot_scales = keep.tile([P, 2 * P], U8, align_bytes=64)
        u_codes = keep.tile([P, PACK * P], U32, align_bytes=64)
        u_scales = keep.tile([P, PACK * P], U8, align_bytes=64)
        w_codes = keep.tile([P, PACK * P], U32, align_bytes=64)
        w_scales = keep.tile([P, PACK * P], U8, align_bytes=64)
        q_codes = keep.tile([P, PACK * P], U32, align_bytes=64)
        q_scales = keep.tile([P, PACK * P], U8, align_bytes=64)

        diff_rows = keep.tile([P, PACK, P], F32)
        nc.vector.tensor_tensor(
            out=diff_rows[:],
            in0=slots_sb[:, 1, :].rearrange("m (p t) -> m t p", t=PACK),
            in1=slots_sb[:, 0, :].rearrange("m (p t) -> m t p", t=PACK),
            op=ALU.subtract,
        )

        slots_grouped = keep.tile([P, 2, P, PACK], BF16, align_bytes=64)
        for i in range(2):
            transpose_tile(slots_sb[:, i, :], slots_grouped[:, i, :, :])
        fill_time(P)
        quantise(slots_grouped[:].rearrange("p i r t -> p (i r) t"), slot_codes[:], slot_scales[:])

        u_pairs = [keep.tile([P, 2, P, PACK], BF16, align_bytes=64, name="u_pair%d" % u) for u in range(2)]
        w_pairs = [keep.tile([P, 2, P, PACK], BF16, align_bytes=64, name="w_pair%d" % u) for u in range(2)]

        def quantise_pair(pairs, codes, scales, u):
            pair = slice(2 * u * P, (2 * u + 2) * P)
            quantise(pairs[u][:].rearrange("p i r t -> p (i r) t"), codes[:, pair], scales[:, pair])

        transpose_tile(u_sb[:, 0, :], u_pairs[0][:, 0, :, :])
        transpose_tile(u_sb[:, 1, :], u_pairs[0][:, 1, :, :])
        transpose_tile(w_sb[:, 0, :], w_pairs[0][:, 0, :, :], nc.vector.tensor_copy)
        transpose_tile(w_sb[:, 1, :], w_pairs[0][:, 1, :, :])
        fill_time(96)
        quantise_pair(u_pairs, u_codes, u_scales, 0)
        transpose_tile(u_sb[:, 2, :], u_pairs[1][:, 0, :, :])
        transpose_tile(u_sb[:, 3, :], u_pairs[1][:, 1, :, :])
        quantise_pair(w_pairs, w_codes, w_scales, 0)
        quantise_pair(u_pairs, u_codes, u_scales, 1)
        for t in (2, 3):
            chunk = slice(t * P, (t + 1) * P)
            grouped = w_pairs[1][:, t - 2, :, :]
            transpose_tile(w_sb[:, t, :], grouped)
            quantise(grouped, w_codes[:, chunk], w_scales[:, chunk])

        diff_ps = back_psum.tile([P, PACK, P], F32, tag="back", name="diff_ps")
        for t in range(PACK):
            nc.tensor.transpose(diff_ps[:, t, :], diff_rows[:, t, :], identity[:])

        def gate_passes(gate_ps, i, t):
            chunk = slice(t * P, (t + 1) * P)
            nc.tensor.matmul_mx(
                out=gate_ps[:, i, :],
                lhsT=u_codes[:, chunk].bitcast(FP8X4),
                lhsT_scale=u_scales[:, chunk],
                rhs=slot_codes[:, 0:P].bitcast(FP8X4),
                rhs_scale=slot_scales[:, 0:P],
                start=True,
                stop=False,
            )
            nc.tensor.matmul_mx(
                out=gate_ps[:, i, :],
                lhsT=w_codes[:, chunk].bitcast(FP8X4),
                lhsT_scale=w_scales[:, chunk],
                rhs=slot_codes[:, P : 2 * P].bitcast(FP8X4),
                rhs_scale=slot_scales[:, P : 2 * P],
                start=False,
                stop=True,
            )

        tanh_planes = keep.tile([P, PACK, P], F32)
        step_planes = keep.tile([P, PACK, P], F32)
        q_grouped = [stage.tile([P, P, PACK], BF16, align_bytes=64, name="q_grouped") for j in range(PACK)]
        gates = [half_psum.tile([P, 2, P], F32, tag=name, name="gate_" + name) for name in "abc"]

        def take_tanh(gate_ps, first, last):
            nc.scalar.activation(
                out=tanh_planes[:, first : last + 1, :],
                in_=gate_ps[:, 0 : last - first + 1, :],
                func=ACT.Tanh,
                scale=0.5,
            )

        mnew_grouped = keep.tile([P, P, PACK], BF16, align_bytes=64)
        mnew_codes = keep.tile([P, P], U32, align_bytes=64)
        mnew_scales = keep.tile([P, P], U8, align_bytes=64)

        def take_step(first, last):
            ts = slice(first, last + 1)
            nc.vector.scalar_tensor_tensor(
                out=step_planes[:, ts, :],
                in0=tanh_planes[:, ts, :],
                scalar=1.0,
                in1=diff_ps[:, ts, :],
                op0=ALU.add,
                op1=ALU.mult,
            )

        def blend(u):
            ts = slice(2 * u, 2 * u + 2)
            nc.vector.scalar_tensor_tensor(
                out=mnew_grouped[:, :, ts],
                in0=step_planes[:, ts, :].rearrange("p e m -> p m e"),
                scalar=0.5,
                in1=slots_grouped[:, 0, :, ts],
                op0=ALU.mult,
                op1=ALU.add,
            )

        def quantise_queries(j):
            chunk = slice(j * P, (j + 1) * P)
            quantise(q_grouped[j][:], q_codes[:, chunk], q_scales[:, chunk])

        gate_passes(gates[0], 0, 0)
        gate_passes(gates[0], 1, 1)
        take_tanh(gates[0], 0, 1)
        gate_passes(gates[1], 0, 2)
        take_tanh(gates[1], 2, 2)
        gate_passes(gates[2], 0, 3)
        take_tanh(gates[2], 3, 3)
        for j in range(PACK):
            transpose_tile(q_sb[:, j, :], q_grouped[j][:])
        take_step(0, 1)
        take_step(2, 2)
        take_step(3, 3)
        blend(0)
        blend(1)
        quantise_queries(0)
        quantise(mnew_grouped[:], mnew_codes[:], mnew_scales[:])
        for j in range(1, PACK):
            quantise_queries(j)

        back_ps = back_psum.tile([P, PACK, P], F32, tag="back", name="back_ps")
        for t in range(PACK):
            nc.tensor.transpose(back_ps[:, t, :], step_planes[:, t, :], identity[:])
        half_step = keep.tile([P, D], F32)
        mnew_out = keep.tile([P, D], F32)
        for h in range(2):
            ps = slice(h * P // 2, (h + 1) * P // 2)
            ds = slice(h * D // 2, (h + 1) * D // 2)
            nc.scalar.activation(
                out=half_step[:, ds].rearrange("m (p t) -> m p t", t=PACK),
                in_=back_ps[:, :, ps].rearrange("m t p -> m p t"),
                func=ACT.Copy,
                scale=0.5,
            )
            nc.gpsimd.tensor_tensor(
                out=mnew_out[:, ds], in0=half_step[:, ds], in1=slots_sb[:, 0, ds], op=ALU.add
            )
            nc.sync.dma_start(out=out_0[:, ds], in_=mnew_out[:, ds])

        logit_halves = []
        for h, name in enumerate(("a", "b")):
            logit_ps = half_psum.tile([P, 2, P], F32, tag=name, name="logits_" + name)
            logit_halves.append(logit_ps)
            for i in range(2):
                chunk = slice((2 * h + i) * P, (2 * h + i + 1) * P)
                nc.tensor.matmul_mx(
                    out=logit_ps[:, i, :],
                    lhsT=q_codes[:, chunk].bitcast(FP8X4),
                    lhsT_scale=q_scales[:, chunk],
                    rhs=mnew_codes[:].bitcast(FP8X4),
                    rhs_scale=mnew_scales[:],
                    start=True,
                    stop=True,
                )

        negated = keep.tile([P, PACK, P], F32)
        shift = keep.tile([P, PACK], F32)
        expd = keep.tile([P, PACK, P], F32)
        sums = keep.tile([P, PACK], F32)
        inv_sums = keep.tile([P, PACK], F32)
        w_att = keep.tile([P, PACK, P], F32)
        for j in range(PACK):
            nc.vector.tensor_scalar(
                out=negated[:, j, :],
                in0=logit_halves[j // 2][:, j % 2, :],
                scalar1=-INV_TEMP,
                scalar2=None,
                op0=ALU.mult,
                op1=ALU.min,
                accum_out=shift[:, j : j + 1],
            )
            nc.scalar.activation(
                out=expd[:, j, :],
                in_=negated[:, j, :],
                func=ACT.Exp,
                bias=shift[:, j : j + 1],
                scale=-1.0,
                accum_out=sums[:, j : j + 1],
            )
        out_rows = out_1.rearrange("t b m -> (t b) m").rearrange("(r j) m -> r j m", j=PACK)

        def invert(j):
            nc.vector.reciprocal(out=inv_sums[:, j : j + 1], in_=sums[:, j : j + 1])

        def normalise(j):
            nc.vector.tensor_scalar_mul(out=w_att[:, j, :], in0=expd[:, j, :], scalar1=inv_sums[:, j : j + 1])

        invert(0)
        for j in range(PACK):
            if j + 1 < PACK:
                invert(j + 1)
            normalise(j)
            if j % 2 == 1:
                js = slice(j - 1, j + 1)
                nc.sync.dma_start(out=out_rows[:, js, :], in_=w_att[:, js, :])
